import numpy as np
import ml_dtypes


def mxq(x, axis, fmt="e4m3"):
    dtype, down = {"e4m3": (ml_dtypes.float8_e4m3fn, 7), "e5m2": (ml_dtypes.float8_e5m2, 14)}[fmt]
    v = np.moveaxis(np.asarray(x, np.float32).astype(ml_dtypes.bfloat16).astype(np.float64), axis, -1)
    blocks = v.reshape(v.shape[:-1] + (-1, 32))
    amax = np.abs(blocks).max(-1, keepdims=True)
    byte = np.maximum(np.where(amax > 0, np.frexp(amax)[1] - 1 + 127, 0) - down, 1)
    scale = np.exp2(byte - 127.0)
    codes = (blocks / scale).astype(np.float32).astype(dtype).astype(np.float64)
    return np.moveaxis((codes * scale).reshape(v.shape), -1, axis)


WIDE = False


def mx_kscale(k):
    if not WIDE:
        return np.ones(k)
    levels = np.array([10, -10, 5, -5, 0])
    a = np.random.permutation(np.resize(levels, k // 512 * 4)).reshape(k // 512, 4)
    idx = np.arange(k)
    return np.exp2(a[idx // 512, idx % 128 // 32])


BF16 = ml_dtypes.bfloat16


def bf(x):
    return np.asarray(x, np.float32).astype(BF16)


def f64(x):
    return np.asarray(x).astype(np.float64)


E2M1 = np.array([0.0, 0.5, 1.0, 1.5, 2.0, 3.0, 4.0, 6.0, -0.0, -0.5, -1.0, -1.5, -2.0, -3.0, -4.0, -6.0])


def pack_weight(w, fmt):
    k, n = w.shape
    w = f64(bf(w)).reshape(k // 32, 32, n)
    amax = np.abs(w).max(1)
    if fmt == "e4m3":
        byte = np.frexp(amax)[1] - 1 + 127 - 7
    else:
        mant, ex = np.frexp(amax / 6.0)
        byte = np.where(mant > 0.5, ex, ex - 1) + 127
    byte = np.clip(np.where(amax > 0, byte, 1), 1, 254)
    scaled = (w * np.exp2(127.0 - byte)[:, None, :]).reshape(k, n).astype(np.float32)
    by_word = np.ascontiguousarray(scaled.reshape(k // 512, 128, 4, n).transpose(0, 1, 3, 2))
    if fmt == "e4m3":
        words = by_word.astype(ml_dtypes.float8_e4m3fn).view(np.uint8)
    else:
        c = by_word.astype(ml_dtypes.float4_e2m1fn).view(np.uint8) & 0xF
        words = c[..., 0::2] | (c[..., 1::2] << 4)
    return np.ascontiguousarray(words), np.ascontiguousarray(byte.astype(np.uint8).reshape(k // 512, 16, n))


def unpack_weight(words, scales, fmt):
    g, p, n, _ = words.shape
    if fmt == "e4m3":
        vals = np.ascontiguousarray(words).view(ml_dtypes.float8_e4m3fn).astype(np.float64)
    else:
        nib = np.empty((g, p, n, 4), np.uint8)
        nib[..., 0::2] = words & 0xF
        nib[..., 1::2] = words >> 4
        vals = E2M1[nib]
    vals = vals * np.repeat(np.exp2(scales.astype(np.float64) - 127.0), 8, axis=1)[..., None]
    return vals.transpose(0, 1, 3, 2).reshape(g * 512, n)


D, HIST, HID, N, B = 256, 8, 512, 32, 128
FMIN, FMAX = 0.5, 40.0
TICK_INTERVAL = 0.1
LN_EPS = 1e-5
ERF_CUT, ERF_TERMS = 6.0, 110
FMT = "e4m3"


def erf(v):
    a = np.clip(v, -ERF_CUT, ERF_CUT)
    u = 2.0 * a * a
    acc = np.ones_like(a)
    for k in range(ERF_TERMS, 0, -1):
        acc *= u
        acc /= 2.0 * k + 1.0
        acc += 1.0
    return 2.0 / np.sqrt(np.pi) * a * np.exp(-a * a) * acc


def gelu(v):
    return 0.5 * v * (1.0 + erf(v / np.sqrt(2.0)))


def oscillator(tick):
    i = np.arange(N, dtype=np.float64)
    freq = FMIN * (FMAX / FMIN) ** (i / (N - 1))
    phase = np.mod(i * 2.3571, 2.0 * np.pi)
    t = tick * TICK_INTERVAL
    return 1.0 + 0.5 * np.sin(2.0 * np.pi * freq * t + phase)


def setup_inputs():
    s = mx_kscale(HID)
    h1 = bf(gelu(np.random.standard_normal((B, N, HID))) * s)
    W2 = np.random.standard_normal((N, HID, HID)) * 0.8 / np.sqrt(HID) / s[:, None]
    W2_words, W2_scales = pack_weight(W2.reshape(-1, HID), FMT)
    b2 = bf(np.random.standard_normal((N, HID)) * 0.25)
    W3 = np.random.standard_normal((N, HID, D)) * 1.5 / np.sqrt(HID)
    W3_words, W3_scales = pack_weight(W3.reshape(-1, D), FMT)
    return {"h1": h1,
            "W2_words": W2_words,
            "W2_scales": W2_scales,
            "b2": b2,
            "W3_words": W3_words,
            "W3_scales": W3_scales,
            "b3": bf(np.random.standard_normal((N, D)) * 0.3),
            "gamma": bf(1.0 + 0.1 * np.random.standard_normal((N, D))),
            "beta": bf(np.random.standard_normal((N, D)) * 0.3),
            "tick": 7}


def reference(h1, W2_words, W2_scales, b2, W3_words, W3_scales, b3, gamma, beta, tick):
    a = f64(h1).transpose(1, 0, 2)
    g = gelu((mxq(a, 2, "e4m3") @ unpack_weight(W2_words, W2_scales, FMT).reshape(N, HID, HID)) + f64(b2)[:, None, :])
    y = (mxq(g, 2, "e4m3") @ unpack_weight(W3_words, W3_scales, FMT).reshape(N, HID, D)) + f64(b3)[:, None, :]
    mu = y.mean(-1, keepdims=True)
    var = ((y - mu) ** 2).mean(-1, keepdims=True)
    z = (y - mu) / np.sqrt(var + LN_EPS) * f64(gamma)[:, None, :] + f64(beta)[:, None, :]
    return (z * oscillator(tick)[:, None, None]).transpose(1, 0, 2)

@@ -1,0 +1,356 @@
+import math
+from contextlib import ExitStack
+
+import concourse.mybir as mybir
+from concourse.masks import make_identity
+
+F32 = mybir.dt.float32
+BF16 = mybir.dt.bfloat16
+U8 = mybir.dt.uint8
+U32 = mybir.dt.uint32
+I32 = mybir.dt.int32
+FP8X4 = mybir.dt.float8_e4m3fn_x4
+ALU = mybir.AluOpType
+ACT = mybir.ActivationFunctionType
+
+P = 128
+PACK = 4
+NEURONS = 32
+HID = 512
+FEAT = 256
+LN_EPS = 1e-5
+F_MIN, F_MAX, TICK_INTERVAL = 0.5, 40.0, 0.1
+
+PAIR = 2
+N_PAIRS = NEURONS // PAIR
+CHUNK = 4
+N_CHUNKS = NEURONS // CHUNK
+PLANES = 4
+PLANE_COLS = NEURONS // PLANES
+HALVES = FEAT // P
+SPREAD_STEPS = 4
+
+FLOPS = 2 * P * NEURONS * (HID * HID + HID * FEAT)
+
+
+def sine(x):
+    r = x % (2.0 * math.pi) - math.pi
+    term = r
+    total = r
+    for k in range(1, 20):
+        term = -term * r * r / ((2 * k) * (2 * k + 1))
+        total += term
+    return -total
+
+
+def oscillator_gain(neuron, tick):
+    freq = F_MIN * (F_MAX / F_MIN) ** (neuron / (NEURONS - 1))
+    phase = (neuron * 2.3571) % (2.0 * math.pi)
+    return 1.0 + 0.5 * sine(2.0 * math.pi * freq * (tick * TICK_INTERVAL) + phase)
+
+
+def tile_neuronpool_pa_e_kernel(
+    tc, h1, W2_words, W2_scales, b2, W3_words, W3_scales, b3, gamma, beta, tick, out
+):
+    nc = tc.nc
+    with ExitStack() as stack:
+        const = stack.enter_context(tc.tile_pool(name="const", bufs=1))
+        weights = stack.enter_context(tc.tile_pool(name="weights", bufs=N_CHUNKS))
+        acts = stack.enter_context(tc.tile_pool(name="acts", bufs=4))
+        work = stack.enter_context(tc.tile_pool(name="work", bufs=2))
+        psum = stack.enter_context(tc.psum_pool(name="psum", bufs=1))
+        stack.enter_context(tc.manual_schedule())
+
+        word_rows = const.tile([P, FEAT], BF16)
+        nc.vector.memset(word_rows[96:128, :], 0.0)
+        nc.sync.dma_start(out=word_rows[0:32, :], in_=b3)
+        nc.sync.dma_start(out=word_rows[32:64, :], in_=b2[:, 0:FEAT])
+        nc.sync.dma_start(out=word_rows[64:96, :], in_=b2[:, FEAT:HID])
+        affine_rows = const.tile([P, FEAT], BF16)
+        nc.vector.memset(affine_rows[64:128, :], 0.0)
+        nc.sync.dma_start(out=affine_rows[0:32, :], in_=gamma)
+        nc.sync.dma_start(out=affine_rows[32:64, :], in_=beta)
+
+        w2_planes = const.tile([P, PLANE_COLS, HID], U8, align_bytes=64)
+        w3_planes = const.tile([P, PLANE_COLS, FEAT], U8, align_bytes=64)
+        nc.vector.memset(w2_planes[:].bitcast(I32), 0)
+        nc.vector.memset(w3_planes[:].bitcast(I32), 0)
+        def load_scales(k):
+            group = slice(k * PLANE_COLS, (k + 1) * PLANE_COLS)
+            for r in range(4):
+                nc.sync.dma_start(
+                    out=w2_planes[4 * k + r : P : 32, :, :].bitcast(I32),
+                    in_=W2_scales[group, r:16:4, :].rearrange("g q n -> q g n").bitcast(I32),
+                )
+                nc.sync.dma_start(
+                    out=w3_planes[4 * k + r : P : 32, :, :].bitcast(I32),
+                    in_=W3_scales[group, r:16:4, :].rearrange("g q n -> q g n").bitcast(I32),
+                )
+
+        h1_chunks = []
+        w2_chunks = []
+        w3_chunks = []
+
+        def load_h1(c):
+            h1_sb = acts.tile([P, CHUNK, HID], BF16)
+            nc.sync.dma_start(out=h1_sb[:], in_=h1[:, c * CHUNK : (c + 1) * CHUNK, :])
+            h1_chunks.append(h1_sb)
+
+        def load_weights(c):
+            rows = slice(c * CHUNK, (c + 1) * CHUNK)
+            w2_sb = weights.tile([P, CHUNK, PACK * HID], U8, align_bytes=64)
+            nc.sync.dma_start(
+                out=w2_sb[:].bitcast(I32),
+                in_=W2_words[rows].rearrange("g p n t -> p g (n t)").bitcast(I32),
+            )
+            w3_sb = weights.tile([P, CHUNK, PACK * FEAT], U8, align_bytes=64)
+            nc.sync.dma_start(
+                out=w3_sb[:].bitcast(I32),
+                in_=W3_words[rows].rearrange("g p n t -> p g (n t)").bitcast(I32),
+            )
+            w2_chunks.append(w2_sb)
+            w3_chunks.append(w3_sb)
+
+        load_h1(0)
+        load_scales(0)
+        load_weights(0)
+        for k in range(1, PLANES):
+            load_scales(k)
+        for c in range(1, N_CHUNKS):
+            load_h1(c)
+            load_weights(c)
+
+        ident_f32 = const.tile([P, P], F32)
+        make_identity(nc, ident_f32[:])
+        ident_bf16 = const.tile([P, P], BF16)
+        make_identity(nc, ident_bf16[:])
+        neg_half = const.tile([P, PAIR], F32)
+        nc.vector.memset(neg_half[:], -0.5)
+
+        word_ps = psum.tile([P, P], F32, tag="x2", bufs=2)
+        nc.tensor.transpose(out=word_ps[:], in_=word_rows[:].bitcast(F32), identity=ident_f32[:])
+        word_cols = const.tile([P, P], F32)
+        nc.vector.tensor_copy(out=word_cols[:], in_=word_ps[:])
+        affine_ps = psum.tile([P, HALVES, P], BF16, tag="xT", bufs=2)
+        for half in range(HALVES):
+            nc.tensor.transpose(
+                out=affine_ps[:, half, :],
+                in_=affine_rows[:, half * P : (half + 1) * P],
+                identity=ident_bf16[:],
+            )
+        affine_cols = const.tile([P, HALVES, P], F32)
+        nc.vector.tensor_copy(out=affine_cols[:], in_=affine_ps[:])
+
+        b2_all = const.tile([P, NEURONS, HID], BF16)
+        b3_all = const.tile([P, NEURONS, FEAT], BF16)
+
+        def spread(columns, dest_words, on_vector):
+            bank = psum.tile([P, 4, P], F32, tag="ynT" if on_vector else "z", name="bank")
+            for q, col in enumerate(columns):
+                nc.tensor.transpose(
+                    out=bank[:, q, :],
+                    in_=word_cols[:, col : col + 1].to_broadcast([P, P]),
+                    identity=ident_f32[:],
+                )
+            flat = bank[:].rearrange("p q w -> p (q w)")
+            if on_vector:
+                nc.vector.tensor_copy(out=dest_words, in_=flat)
+            else:
+                nc.scalar.copy(out=dest_words, in_=flat)
+
+        def words_of(tile_slice):
+            return tile_slice.rearrange("p n j -> p (n j)").bitcast(F32)
+
+        def spread_chunk(c):
+            first = c * CHUNK
+            for n in (first, first + PAIR):
+                spread(
+                    [32 + n, 64 + n, 32 + n + 1, 64 + n + 1],
+                    words_of(b2_all[:, n : n + PAIR, :]),
+                    on_vector=(n % CHUNK == 0),
+                )
+            spread(
+                [first, first + 1, first + 2, first + 3],
+                words_of(b3_all[:, first : first + CHUNK, :]),
+                on_vector=(c % 2 == 0),
+            )
+
+        a_ops = {}
+        x_biased = {}
+        g_grouped = {}
+        g_ops = {}
+        moments = {}
+        y_norm = {}
+        z_cols = {}
+        out_tiles = {}
+
+        def quantise_h1(i):
+            h1_sb = h1_chunks[i // 2]
+            a_ps = psum.tile([P, PAIR, 2, P], F32, tag="aT")
+            for j in range(PAIR):
+                words = h1_sb[:, (i % 2) * PAIR + j, :].bitcast(F32)
+                for u in range(2):
+                    nc.tensor.transpose(
+                        out=a_ps[:, j, u, :], in_=words[:, u : HID // 2 : 2], identity=ident_f32[:]
+                    )
+            a_grouped = work.tile([P, PAIR * HID], BF16, align_bytes=64)
+            nc.scalar.copy(
+                out=a_grouped[:].bitcast(F32).rearrange("p (j b u) -> p j b u", j=PAIR, u=2),
+                in_=a_ps[:].rearrange("p j u b -> p j b u"),
+            )
+            a_codes = work.tile([P, PAIR * P], U32, align_bytes=64, bufs=3)
+            a_scales = work.tile([P, PAIR * P], U8, align_bytes=64, bufs=3)
+            nc.vector.quantize_mx(out=a_codes[:].bitcast(FP8X4), scales=a_scales[:], in_=a_grouped[:])
+            a_ops[i] = (a_codes, a_scales)
+
+        def layer2(i):
+            a_codes, a_scales = a_ops[i]
+            xb = work.tile([P, PAIR, PACK, P], F32)
+            for j in range(PAIR):
+                n = i * PAIR + j
+                rows = slice(j * P, (j + 1) * P)
+                x2 = psum.tile([P, HID], F32, tag="x2", bufs=2)
+                nc.tensor.matmul_mx(
+                    out=x2[:],
+                    lhsT=a_codes[:, rows].bitcast(FP8X4),
+                    lhsT_scale=a_scales[:, rows],
+                    rhs=w2_chunks[n // CHUNK][:, n % CHUNK, :].bitcast(FP8X4),
+                    rhs_scale=w2_planes[4 * (n // PLANE_COLS) : P, n % PLANE_COLS, :],
+                    start=True,
+                    stop=True,
+                )
+                nc.vector.tensor_tensor(
+                    out=xb[:, j, :, :],
+                    in0=x2[:].rearrange("b (p t) -> b t p", t=PACK),
+                    in1=b2_all[:, n, :].rearrange("b (p t) -> b t p", t=PACK),
+                    op=ALU.add,
+                )
+            x_biased[i] = xb
+
+        def gelu_transposed(i):
+            xb = x_biased[i]
+            gg = work.tile([P, PAIR, P, PACK], BF16, align_bytes=64)
+            for j in range(PAIR):
+                x_ps = psum.tile([P, PACK, P], F32, tag="xT", bufs=2)
+                for t in range(PACK):
+                    nc.tensor.transpose(out=x_ps[:, t, :], in_=xb[:, j, t, :], identity=ident_f32[:])
+                nc.scalar.activation(
+                    out=gg[:, j, :, :], in_=x_ps[:].rearrange("p t b -> p b t"), func=ACT.Gelu
+                )
+            g_grouped[i] = gg
+
+        def quantise_g(i):
+            g_codes = work.tile([P, PAIR * P], U32, align_bytes=64)
+            g_scales = work.tile([P, PAIR * P], U8, align_bytes=64)
+            nc.vector.quantize_mx(
+                out=g_codes[:].bitcast(FP8X4),
+                scales=g_scales[:],
+                in_=g_grouped[i][:].rearrange("p j b t -> p (j b t)"),
+            )
+            g_ops[i] = (g_codes, g_scales)
+
+        def layer3_and_moments(i):
+            g_codes, g_scales = g_ops[i]
+            x3 = psum.tile([P, PAIR, FEAT], F32, tag="x3")
+            for j in range(PAIR):
+                n = i * PAIR + j
+                rows = slice(j * P, (j + 1) * P)
+                nc.tensor.matmul_mx(
+                    out=x3[:, j, :],
+                    lhsT=g_codes[:, rows].bitcast(FP8X4),
+                    lhsT_scale=g_scales[:, rows],
+                    rhs=w3_chunks[n // CHUNK][:, n % CHUNK, :].bitcast(FP8X4),
+                    rhs_scale=w3_planes[4 * (n // PLANE_COLS) : P, n % PLANE_COLS, :],
+                    start=True,
+                    stop=True,
+                )
+            y = work.tile([P, PAIR, FEAT], F32, bufs=3)
+            nc.vector.tensor_tensor(
+                out=y[:], in0=x3[:], in1=b3_all[:, i * PAIR : (i + 1) * PAIR, :], op=ALU.add
+            )
+            stats = work.tile([P, PAIR, 6], F32, bufs=3)
+            mean_var = work.tile([P, PAIR, 2], F32, bufs=3)
+            for j in range(PAIR):
+                nc.vector.bn_stats(out=stats[:, j, :], in_=y[:, j, :])
+                nc.vector.bn_aggr(out=mean_var[:, j, :], in_=stats[:, j, :])
+            var_eps = work.tile([P, PAIR], F32, bufs=3)
+            nc.gpsimd.tensor_scalar_add(out=var_eps[:], in0=mean_var[:, :, 1], scalar1=LN_EPS)
+            rstd = work.tile([P, PAIR], F32, bufs=3)
+            nc.gpsimd.tensor_tensor(out=rstd[:], in0=var_eps[:], in1=neg_half[:], op=ALU.pow)
+            moments[i] = (y, mean_var, rstd)
+
+        def normalise(i):
+            y, mean_var, rstd = moments[i]
+            yn = work.tile([P, PAIR, FEAT], F32)
+            for j in range(PAIR):
+                nc.vector.tensor_scalar(
+                    out=yn[:, j, :],
+                    in0=y[:, j, :],
+                    scalar1=mean_var[:, j, 0:1],
+                    scalar2=rstd[:, j : j + 1],
+                    op0=ALU.subtract,
+                    op1=ALU.mult,
+                )
+            y_norm[i] = yn
+
+        def scale_and_shift(i):
+            yn = y_norm[i]
+            yn_ps = psum.tile([P, PAIR, HALVES, P], F32, tag="ynT")
+            zc = work.tile([P, PAIR, HALVES, P], F32)
+            for j in range(PAIR):
+                for half in range(HALVES):
+                    nc.tensor.transpose(
+                        out=yn_ps[:, j, half, :],
+                        in_=yn[:, j, half * P : (half + 1) * P],
+                        identity=ident_f32[:],
+                    )
+            for j in range(PAIR):
+                n = i * PAIR + j
+                for half in range(HALVES):
+                    nc.scalar.activation(
+                        out=zc[:, j, half, :],
+                        in_=yn_ps[:, j, half, :],
+                        func=ACT.Identity,
+                        scale=affine_cols[:, half, n : n + 1],
+                        bias=affine_cols[:, half, 32 + n : 32 + n + 1],
+                    )
+            z_cols[i] = zc
+
+        def gain_and_store(i):
+            zc = z_cols[i]
+            c = i // 2
+            if i % 2 == 0:
+                out_sb = work.tile([P, CHUNK, FEAT], F32, bufs=3)
+                out_tiles[c] = out_sb
+            z_ps = psum.tile([P, PAIR, FEAT], F32, tag="z")
+            for j in range(PAIR):
+                for half in range(HALVES):
+                    nc.tensor.transpose(
+                        out=z_ps[:, j, half * P : (half + 1) * P],
+                        in_=zc[:, j, half, :],
+                        identity=ident_f32[:],
+                    )
+            for j in range(PAIR):
+                n = i * PAIR + j
+                nc.scalar.mul(
+                    out=out_tiles[c][:, n % CHUNK, :], in_=z_ps[:, j, :], mul=oscillator_gain(n, tick)
+                )
+            if i % 2 == 1:
+                nc.scalar.dma_start(out=out[:, c * CHUNK : (c + 1) * CHUNK, :], in_=out_tiles[c][:])
+
+        def run(stage, i):
+            if 0 <= i < N_PAIRS:
+                stage(i)
+
+        for step in range(N_PAIRS + 7):
+            run(quantise_g, step - 3)
+            run(normalise, step - 5)
+            if step < SPREAD_STEPS:
+                for c in range(step * N_CHUNKS // SPREAD_STEPS, (step + 1) * N_CHUNKS // SPREAD_STEPS):
+                    spread_chunk(c)
+            run(quantise_h1, step)
+            run(gain_and_store, step - 7)
+            run(scale_and_shift, step - 6)
+            run(gelu_transposed, step - 2)
+            run(layer2, step - 1)
+            run(layer3_and_moments, step - 3)

@@ -28,7 +28,6 @@ N_CHUNKS = NEURONS // CHUNK
 PLANES = 4
 PLANE_COLS = NEURONS // PLANES
 HALVES = FEAT // P
-SPREAD_STEPS = 4
 
 FLOPS = 2 * P * NEURONS * (HID * HID + HID * FEAT)
 
@@ -61,11 +60,6 @@ def tile_neuronpool_pa_e_kernel(
         psum = stack.enter_context(tc.psum_pool(name="psum", bufs=1))
         stack.enter_context(tc.manual_schedule())
 
-        word_rows = const.tile([P, FEAT], BF16)
-        nc.vector.memset(word_rows[96:128, :], 0.0)
-        nc.sync.dma_start(out=word_rows[0:32, :], in_=b3)
-        nc.sync.dma_start(out=word_rows[32:64, :], in_=b2[:, 0:FEAT])
-        nc.sync.dma_start(out=word_rows[64:96, :], in_=b2[:, FEAT:HID])
         affine_rows = const.tile([P, FEAT], BF16)
         nc.vector.memset(affine_rows[64:128, :], 0.0)
         nc.sync.dma_start(out=affine_rows[0:32, :], in_=gamma)
@@ -111,14 +105,31 @@ def tile_neuronpool_pa_e_kernel(
             w2_chunks.append(w2_sb)
             w3_chunks.append(w3_sb)
 
+        b2_all = const.tile([P, NEURONS, HID], BF16)
+        b3_all = const.tile([P, NEURONS, FEAT], BF16)
+
+        def load_biases(k):
+            group = slice(k * PLANE_COLS, (k + 1) * PLANE_COLS)
+            nc.sync.dma_start(
+                out=b2_all[:, group, :].rearrange("p n j -> p (n j)"),
+                in_=b2[group, :].rearrange("n j -> (n j)").partition_broadcast(P),
+            )
+            nc.sync.dma_start(
+                out=b3_all[:, group, :].rearrange("p n d -> p (n d)"),
+                in_=b3[group, :].rearrange("n d -> (n d)").partition_broadcast(P),
+            )
+
         load_h1(0)
         load_scales(0)
         load_weights(0)
+        load_biases(0)
         for k in range(1, PLANES):
             load_scales(k)
         for c in range(1, N_CHUNKS):
             load_h1(c)
             load_weights(c)
+            if c % 2 == 1 and c < N_CHUNKS - 1:
+                load_biases((c + 1) // 2)
 
         ident_f32 = const.tile([P, P], F32)
         make_identity(nc, ident_f32[:])
@@ -127,10 +138,6 @@ def tile_neuronpool_pa_e_kernel(
         neg_half = const.tile([P, PAIR], F32)
         nc.vector.memset(neg_half[:], -0.5)
 
-        word_ps = psum.tile([P, P], F32, tag="x2", bufs=2)
-        nc.tensor.transpose(out=word_ps[:], in_=word_rows[:].bitcast(F32), identity=ident_f32[:])
-        word_cols = const.tile([P, P], F32)
-        nc.vector.tensor_copy(out=word_cols[:], in_=word_ps[:])
         affine_ps = psum.tile([P, HALVES, P], BF16, tag="xT", bufs=2)
         for half in range(HALVES):
             nc.tensor.transpose(
@@ -140,40 +147,6 @@ def tile_neuronpool_pa_e_kernel(
             )
         affine_cols = const.tile([P, HALVES, P], F32)
         nc.vector.tensor_copy(out=affine_cols[:], in_=affine_ps[:])
-
-        b2_all = const.tile([P, NEURONS, HID], BF16)
-        b3_all = const.tile([P, NEURONS, FEAT], BF16)
-
-        def spread(columns, dest_words, on_vector):
-            bank = psum.tile([P, 4, P], F32, tag="ynT" if on_vector else "z", name="bank")
-            for q, col in enumerate(columns):
-                nc.tensor.transpose(
-                    out=bank[:, q, :],
-                    in_=word_cols[:, col : col + 1].to_broadcast([P, P]),
-                    identity=ident_f32[:],
-                )
-            flat = bank[:].rearrange("p q w -> p (q w)")
-            if on_vector:
-                nc.vector.tensor_copy(out=dest_words, in_=flat)
-            else:
-                nc.scalar.copy(out=dest_words, in_=flat)
-
-        def words_of(tile_slice):
-            return tile_slice.rearrange("p n j -> p (n j)").bitcast(F32)
-
-        def spread_chunk(c):
-            first = c * CHUNK
-            for n in (first, first + PAIR):
-                spread(
-                    [32 + n, 64 + n, 32 + n + 1, 64 + n + 1],
-                    words_of(b2_all[:, n : n + PAIR, :]),
-                    on_vector=(n % CHUNK == 0),
-                )
-            spread(
-                [first, first + 1, first + 2, first + 3],
-                words_of(b3_all[:, first : first + CHUNK, :]),
-                on_vector=(c % 2 == 0),
-            )
 
         a_ops = {}
         x_biased = {}
@@ -345,9 +318,6 @@ def tile_neuronpool_pa_e_kernel(
         for step in range(N_PAIRS + 7):
             run(quantise_g, step - 3)
             run(normalise, step - 5)
-            if step < SPREAD_STEPS:
-                for c in range(step * N_CHUNKS // SPREAD_STEPS, (step + 1) * N_CHUNKS // SPREAD_STEPS):
-                    spread_chunk(c)
             run(quantise_h1, step)
             run(gain_and_store, step - 7)
             run(scale_and_shift, step - 6)

@@ -152,6 +152,8 @@ def tile_neuronpool_pa_e_kernel(
         x_biased = {}
         g_grouped = {}
         g_ops = {}
+        y_biased = {}
+        y_stats = {}
         moments = {}
         y_norm = {}
         z_cols = {}
@@ -222,7 +224,7 @@ def tile_neuronpool_pa_e_kernel(
             )
             g_ops[i] = (g_codes, g_scales)
 
-        def layer3_and_moments(i):
+        def layer3(i):
             g_codes, g_scales = g_ops[i]
             x3 = psum.tile([P, PAIR, FEAT], F32, tag="x3")
             for j in range(PAIR):
@@ -241,11 +243,19 @@ def tile_neuronpool_pa_e_kernel(
             nc.vector.tensor_tensor(
                 out=y[:], in0=x3[:], in1=b3_all[:, i * PAIR : (i + 1) * PAIR, :], op=ALU.add
             )
+            y_biased[i] = y
+
+        def statistics(i):
             stats = work.tile([P, PAIR, 6], F32, bufs=3)
+            for j in range(PAIR):
+                nc.vector.bn_stats(out=stats[:, j, :], in_=y_biased[i][:, j, :])
+            y_stats[i] = stats
+
+        def aggregate(i):
+            y = y_biased[i]
             mean_var = work.tile([P, PAIR, 2], F32, bufs=3)
             for j in range(PAIR):
-                nc.vector.bn_stats(out=stats[:, j, :], in_=y[:, j, :])
-                nc.vector.bn_aggr(out=mean_var[:, j, :], in_=stats[:, j, :])
+                nc.vector.bn_aggr(out=mean_var[:, j, :], in_=y_stats[i][:, j, :])
             var_eps = work.tile([P, PAIR], F32, bufs=3)
             nc.gpsimd.tensor_scalar_add(out=var_eps[:], in0=mean_var[:, :, 1], scalar1=LN_EPS)
             rstd = work.tile([P, PAIR], F32, bufs=3)
@@ -317,10 +327,12 @@ def tile_neuronpool_pa_e_kernel(
 
         for step in range(N_PAIRS + 7):
             run(quantise_g, step - 3)
+            run(aggregate, step - 4)
             run(normalise, step - 5)
             run(quantise_h1, step)
             run(gain_and_store, step - 7)
             run(scale_and_shift, step - 6)
             run(gelu_transposed, step - 2)
+            run(layer3, step - 3)
             run(layer2, step - 1)
-            run(layer3_and_moments, step - 3)
+            run(statistics, step - 3)

@@ -28,6 +28,8 @@ N_CHUNKS = NEURONS // CHUNK
 PLANES = 4
 PLANE_COLS = NEURONS // PLANES
 HALVES = FEAT // P
+SPREAD_AHEAD = 6
+SPREAD_A_STEP = 3
 
 FLOPS = 2 * P * NEURONS * (HID * HID + HID * FEAT)
 
@@ -60,6 +62,17 @@ def tile_neuronpool_pa_e_kernel(
         psum = stack.enter_context(tc.psum_pool(name="psum", bufs=1))
         stack.enter_context(tc.manual_schedule())
 
+        ident_f32 = const.tile([P, P], F32)
+        make_identity(nc, ident_f32[:])
+        ident_bf16 = const.tile([P, P], BF16)
+        make_identity(nc, ident_bf16[:])
+        neg_half = const.tile([P, PAIR], F32)
+        nc.vector.memset(neg_half[:], -0.5)
+
+        bias_rows = const.tile([P, FEAT], BF16)
+        nc.vector.memset(bias_rows[96:128, :], 0.0)
+        nc.sync.dma_start(out=bias_rows[0:64, :], in_=b2.rearrange("n (k j) -> (n k) j", k=2))
+        nc.sync.dma_start(out=bias_rows[64:96, :], in_=b3)
         affine_rows = const.tile([P, FEAT], BF16)
         nc.vector.memset(affine_rows[64:128, :], 0.0)
         nc.sync.dma_start(out=affine_rows[0:32, :], in_=gamma)
@@ -69,17 +82,15 @@ def tile_neuronpool_pa_e_kernel(
         w3_planes = const.tile([P, PLANE_COLS, FEAT], U8, align_bytes=64)
         nc.vector.memset(w2_planes[:].bitcast(I32), 0)
         nc.vector.memset(w3_planes[:].bitcast(I32), 0)
-        def load_scales(k):
-            group = slice(k * PLANE_COLS, (k + 1) * PLANE_COLS)
+
+        def load_scales(planes, scales):
             for r in range(4):
-                nc.sync.dma_start(
-                    out=w2_planes[4 * k + r : P : 32, :, :].bitcast(I32),
-                    in_=W2_scales[group, r:16:4, :].rearrange("g q n -> q g n").bitcast(I32),
-                )
-                nc.sync.dma_start(
-                    out=w3_planes[4 * k + r : P : 32, :, :].bitcast(I32),
-                    in_=W3_scales[group, r:16:4, :].rearrange("g q n -> q g n").bitcast(I32),
-                )
+                for k in range(PLANES):
+                    group = slice(k * PLANE_COLS, (k + 1) * PLANE_COLS)
+                    nc.sync.dma_start(
+                        out=planes[4 * k + r : P : 32, :, :].bitcast(I32),
+                        in_=scales[group, r:16:4, :].rearrange("g q n -> q g n").bitcast(I32),
+                    )
 
         h1_chunks = []
         w2_chunks = []
@@ -105,38 +116,13 @@ def tile_neuronpool_pa_e_kernel(
             w2_chunks.append(w2_sb)
             w3_chunks.append(w3_sb)
 
-        b2_all = const.tile([P, NEURONS, HID], BF16)
-        b3_all = const.tile([P, NEURONS, FEAT], BF16)
-
-        def load_biases(k):
-            group = slice(k * PLANE_COLS, (k + 1) * PLANE_COLS)
-            nc.sync.dma_start(
-                out=b2_all[:, group, :].rearrange("p n j -> p (n j)"),
-                in_=b2[group, :].rearrange("n j -> (n j)").partition_broadcast(P),
-            )
-            nc.sync.dma_start(
-                out=b3_all[:, group, :].rearrange("p n d -> p (n d)"),
-                in_=b3[group, :].rearrange("n d -> (n d)").partition_broadcast(P),
-            )
-
         load_h1(0)
-        load_scales(0)
+        load_scales(w2_planes, W2_scales)
+        load_scales(w3_planes, W3_scales)
         load_weights(0)
-        load_biases(0)
-        for k in range(1, PLANES):
-            load_scales(k)
         for c in range(1, N_CHUNKS):
             load_h1(c)
             load_weights(c)
-            if c % 2 == 1 and c < N_CHUNKS - 1:
-                load_biases((c + 1) // 2)
-
-        ident_f32 = const.tile([P, P], F32)
-        make_identity(nc, ident_f32[:])
-        ident_bf16 = const.tile([P, P], BF16)
-        make_identity(nc, ident_bf16[:])
-        neg_half = const.tile([P, PAIR], F32)
-        nc.vector.memset(neg_half[:], -0.5)
 
         affine_ps = psum.tile([P, HALVES, P], BF16, tag="xT", bufs=2)
         for half in range(HALVES):
@@ -148,12 +134,44 @@ def tile_neuronpool_pa_e_kernel(
         affine_cols = const.tile([P, HALVES, P], F32)
         nc.vector.tensor_copy(out=affine_cols[:], in_=affine_ps[:])
 
+        bias_ps = psum.tile([P, PACK, P], F32, tag="xT", bufs=2)
+        nc.tensor.transpose(out=bias_ps[:, 0, :], in_=bias_rows[:].bitcast(F32), identity=ident_f32[:])
+        bias_cols = const.tile([P, P], F32)
+        nc.vector.tensor_copy(out=bias_cols[:], in_=bias_ps[:, 0, :])
+        b2_all = const.tile([P, NEURONS, HID], BF16)
+        b3_all = const.tile([P, NEURONS, FEAT], BF16)
+
+        def spread(first_row, target, turn):
+            spread_ps = psum.tile([P, PACK, P], F32, tag=("z", "ynT")[turn % 2])
+            for q in range(PACK):
+                nc.tensor.transpose(
+                    out=spread_ps[:, q, :],
+                    in_=bias_cols[:, first_row + q : first_row + q + 1].to_broadcast([P, P]),
+                    identity=ident_f32[:],
+                )
+            words = target.bitcast(F32).rearrange("p n w -> p (n w)")
+            if turn % 2 == 0:
+                nc.scalar.copy(out=words, in_=spread_ps[:].rearrange("p q w -> p (q w)"))
+            else:
+                nc.vector.tensor_copy(out=words, in_=spread_ps[:].rearrange("p q w -> p (q w)"))
+
+        spreads = []
+        for c in range(N_CHUNKS):
+            for i in (2 * c, 2 * c + 1):
+                spreads.append((PACK * i, b2_all[:, PAIR * i : PAIR * (i + 1), :]))
+            spreads.append((64 + CHUNK * c, b3_all[:, CHUNK * c : CHUNK * (c + 1), :]))
+
+        def spread_some(first, count):
+            for turn in range(first, min(first + count, len(spreads))):
+                spread(spreads[turn][0], spreads[turn][1], turn)
+
+        spread_some(0, SPREAD_AHEAD)
+
         a_ops = {}
         x_biased = {}
         g_grouped = {}
         g_ops = {}
         y_biased = {}
-        y_stats = {}
         moments = {}
         y_norm = {}
         z_cols = {}
@@ -246,30 +264,31 @@ def tile_neuronpool_pa_e_kernel(
             y_biased[i] = y
 
         def statistics(i):
-            stats = work.tile([P, PAIR, 6], F32, bufs=3)
-            for j in range(PAIR):
-                nc.vector.bn_stats(out=stats[:, j, :], in_=y_biased[i][:, j, :])
-            y_stats[i] = stats
-
-        def aggregate(i):
-            y = y_biased[i]
-            mean_var = work.tile([P, PAIR, 2], F32, bufs=3)
-            for j in range(PAIR):
-                nc.vector.bn_aggr(out=mean_var[:, j, :], in_=y_stats[i][:, j, :])
+            stats = work.tile([P, PAIR, 3], F32, bufs=3)
+            nc.vector.bn_stats(
+                out=stats[:].rearrange("p j s -> p (j s)"), in_=y_biased[i][:].rearrange("p j d -> p d j")
+            )
             var_eps = work.tile([P, PAIR], F32, bufs=3)
-            nc.gpsimd.tensor_scalar_add(out=var_eps[:], in0=mean_var[:, :, 1], scalar1=LN_EPS)
+            nc.gpsimd.tensor_scalar(
+                out=var_eps[:],
+                in0=stats[:, :, 2],
+                scalar1=1.0 / FEAT,
+                scalar2=LN_EPS,
+                op0=ALU.mult,
+                op1=ALU.add,
+            )
             rstd = work.tile([P, PAIR], F32, bufs=3)
             nc.gpsimd.tensor_tensor(out=rstd[:], in0=var_eps[:], in1=neg_half[:], op=ALU.pow)
-            moments[i] = (y, mean_var, rstd)
+            moments[i] = (y_biased[i], stats, rstd)
 
         def normalise(i):
-            y, mean_var, rstd = moments[i]
+            y, stats, rstd = moments[i]
             yn = work.tile([P, PAIR, FEAT], F32)
             for j in range(PAIR):
                 nc.vector.tensor_scalar(
                     out=yn[:, j, :],
                     in0=y[:, j, :],
-                    scalar1=mean_var[:, j, 0:1],
+                    scalar1=stats[:, j, 1:2],
                     scalar2=rstd[:, j : j + 1],
                     op0=ALU.subtract,
                     op1=ALU.mult,
@@ -327,7 +346,6 @@ def tile_neuronpool_pa_e_kernel(
 
         for step in range(N_PAIRS + 7):
             run(quantise_g, step - 3)
-            run(aggregate, step - 4)
             run(normalise, step - 5)
             run(quantise_h1, step)
             run(gain_and_store, step - 7)
@@ -336,3 +354,4 @@ def tile_neuronpool_pa_e_kernel(
             run(layer3, step - 3)
             run(layer2, step - 1)
             run(statistics, step - 3)
+            spread_some(SPREAD_AHEAD + SPREAD_A_STEP * step, SPREAD_A_STEP)

@@ -28,8 +28,8 @@ N_CHUNKS = NEURONS // CHUNK
 PLANES = 4
 PLANE_COLS = NEURONS // PLANES
 HALVES = FEAT // P
-SPREAD_AHEAD = 6
-SPREAD_A_STEP = 3
+SPREAD_AHEAD = 12
+SPREAD_A_STEP = 2
 
 FLOPS = 2 * P * NEURONS * (HID * HID + HID * FEAT)
 
@@ -70,9 +70,8 @@ def tile_neuronpool_pa_e_kernel(
         nc.vector.memset(neg_half[:], -0.5)
 
         bias_rows = const.tile([P, FEAT], BF16)
-        nc.vector.memset(bias_rows[96:128, :], 0.0)
+        nc.vector.memset(bias_rows[64:128, :], 0.0)
         nc.sync.dma_start(out=bias_rows[0:64, :], in_=b2.rearrange("n (k j) -> (n k) j", k=2))
-        nc.sync.dma_start(out=bias_rows[64:96, :], in_=b3)
         affine_rows = const.tile([P, FEAT], BF16)
         nc.vector.memset(affine_rows[64:128, :], 0.0)
         nc.sync.dma_start(out=affine_rows[0:32, :], in_=gamma)
@@ -101,28 +100,51 @@ def tile_neuronpool_pa_e_kernel(
             nc.sync.dma_start(out=h1_sb[:], in_=h1[:, c * CHUNK : (c + 1) * CHUNK, :])
             h1_chunks.append(h1_sb)
 
-        def load_weights(c):
-            rows = slice(c * CHUNK, (c + 1) * CHUNK)
+        def load_w2(c, pieces=1):
             w2_sb = weights.tile([P, CHUNK, PACK * HID], U8, align_bytes=64)
-            nc.sync.dma_start(
-                out=w2_sb[:].bitcast(I32),
-                in_=W2_words[rows].rearrange("g p n t -> p g (n t)").bitcast(I32),
-            )
+            size = CHUNK // pieces
+            for first in range(0, CHUNK, size):
+                nc.sync.dma_start(
+                    out=w2_sb[:, first : first + size, :].bitcast(I32),
+                    in_=W2_words[c * CHUNK + first : c * CHUNK + first + size]
+                    .rearrange("g p n t -> p g (n t)")
+                    .bitcast(I32),
+                )
+            w2_chunks.append(w2_sb)
+
+        def load_w3(c):
+            rows = slice(c * CHUNK, (c + 1) * CHUNK)
             w3_sb = weights.tile([P, CHUNK, PACK * FEAT], U8, align_bytes=64)
             nc.sync.dma_start(
                 out=w3_sb[:].bitcast(I32),
                 in_=W3_words[rows].rearrange("g p n t -> p g (n t)").bitcast(I32),
             )
-            w2_chunks.append(w2_sb)
             w3_chunks.append(w3_sb)
+
+        def load_weights(c):
+            load_w2(c)
+            load_w3(c)
+
+        b3_all = const.tile([P, NEURONS, FEAT], BF16)
+
+        def load_b3(k):
+            group = slice(k * PLANE_COLS, (k + 1) * PLANE_COLS)
+            nc.sync.dma_start(
+                out=b3_all[:, group, :].rearrange("p n d -> p (n d)"),
+                in_=b3[group, :].rearrange("n d -> (n d)").partition_broadcast(P),
+            )
 
         load_h1(0)
         load_scales(w2_planes, W2_scales)
+        load_w2(0, pieces=2)
         load_scales(w3_planes, W3_scales)
-        load_weights(0)
+        load_w3(0)
+        load_b3(0)
         for c in range(1, N_CHUNKS):
             load_h1(c)
             load_weights(c)
+            if c % 2 == 1 and c < N_CHUNKS - 1:
+                load_b3((c + 1) // 2)
 
         affine_ps = psum.tile([P, HALVES, P], BF16, tag="xT", bufs=2)
         for half in range(HALVES):
@@ -139,7 +161,6 @@ def tile_neuronpool_pa_e_kernel(
         bias_cols = const.tile([P, P], F32)
         nc.vector.tensor_copy(out=bias_cols[:], in_=bias_ps[:, 0, :])
         b2_all = const.tile([P, NEURONS, HID], BF16)
-        b3_all = const.tile([P, NEURONS, FEAT], BF16)
 
         def spread(first_row, target, turn):
             spread_ps = psum.tile([P, PACK, P], F32, tag=("z", "ynT")[turn % 2])
@@ -159,7 +180,6 @@ def tile_neuronpool_pa_e_kernel(
         for c in range(N_CHUNKS):
             for i in (2 * c, 2 * c + 1):
                 spreads.append((PACK * i, b2_all[:, PAIR * i : PAIR * (i + 1), :]))
-            spreads.append((64 + CHUNK * c, b3_all[:, CHUNK * c : CHUNK * (c + 1), :]))
 
         def spread_some(first, count):
             for turn in range(first, min(first + count, len(spreads))):

@@ -366,12 +366,12 @@ def tile_neuronpool_pa_e_kernel(
 
         for step in range(N_PAIRS + 7):
             run(quantise_g, step - 3)
+            run(statistics, step - 4)
             run(normalise, step - 5)
             run(quantise_h1, step)
             run(gain_and_store, step - 7)
             run(scale_and_shift, step - 6)
             run(gelu_transposed, step - 2)
-            run(layer3, step - 3)
             run(layer2, step - 1)
-            run(statistics, step - 3)
+            run(layer3, step - 3)
             spread_some(SPREAD_AHEAD + SPREAD_A_STEP * step, SPREAD_A_STEP)

import math
from contextlib import ExitStack

import concourse.mybir as mybir
from concourse.masks import make_identity

F32 = mybir.dt.float32
BF16 = mybir.dt.bfloat16
U8 = mybir.dt.uint8
U32 = mybir.dt.uint32
I32 = mybir.dt.int32
FP8X4 = mybir.dt.float8_e4m3fn_x4
ALU = mybir.AluOpType
ACT = mybir.ActivationFunctionType

P = 128
PACK = 4
NEURONS = 32
HID = 512
FEAT = 256
LN_EPS = 1e-5
F_MIN, F_MAX, TICK_INTERVAL = 0.5, 40.0, 0.1

PAIR = 2
N_PAIRS = NEURONS // PAIR
CHUNK = 4
N_CHUNKS = NEURONS // CHUNK
PLANES = 4
PLANE_COLS = NEURONS // PLANES
HALVES = FEAT // P
SPREAD_AHEAD = 12
SPREAD_A_STEP = 2

FLOPS = 2 * P * NEURONS * (HID * HID + HID * FEAT)


def sine(x):
    r = x % (2.0 * math.pi) - math.pi
    term = r
    total = r
    for k in range(1, 20):
        term = -term * r * r / ((2 * k) * (2 * k + 1))
        total += term
    return -total


def oscillator_gain(neuron, tick):
    freq = F_MIN * (F_MAX / F_MIN) ** (neuron / (NEURONS - 1))
    phase = (neuron * 2.3571) % (2.0 * math.pi)
    return 1.0 + 0.5 * sine(2.0 * math.pi * freq * (tick * TICK_INTERVAL) + phase)


def tile_neuronpool_pa_e_kernel(
    tc, h1, W2_words, W2_scales, b2, W3_words, W3_scales, b3, gamma, beta, tick, out
):
    nc = tc.nc
    with ExitStack() as stack:
        const = stack.enter_context(tc.tile_pool(name="const", bufs=1))
        weights = stack.enter_context(tc.tile_pool(name="weights", bufs=N_CHUNKS))
        acts = stack.enter_context(tc.tile_pool(name="acts", bufs=4))
        work = stack.enter_context(tc.tile_pool(name="work", bufs=2))
        psum = stack.enter_context(tc.psum_pool(name="psum", bufs=1))
        stack.enter_context(tc.manual_schedule())

        ident_f32 = const.tile([P, P], F32)
        make_identity(nc, ident_f32[:])
        ident_bf16 = const.tile([P, P], BF16)
        make_identity(nc, ident_bf16[:])
        neg_half = const.tile([P, PAIR], F32)
        nc.vector.memset(neg_half[:], -0.5)

        bias_rows = const.tile([P, FEAT], BF16)
        nc.vector.memset(bias_rows[64:128, :], 0.0)
        nc.sync.dma_start(out=bias_rows[0:64, :], in_=b2.rearrange("n (k j) -> (n k) j", k=2))
        affine_rows = const.tile([P, FEAT], BF16)
        nc.vector.memset(affine_rows[64:128, :], 0.0)
        nc.sync.dma_start(out=affine_rows[0:32, :], in_=gamma)
        nc.sync.dma_start(out=affine_rows[32:64, :], in_=beta)

        w2_planes = const.tile([P, PLANE_COLS, HID], U8, align_bytes=64)
        w3_planes = const.tile([P, PLANE_COLS, FEAT], U8, align_bytes=64)
        nc.vector.memset(w2_planes[:].bitcast(I32), 0)
        nc.vector.memset(w3_planes[:].bitcast(I32), 0)

        def load_scales(planes, scales):
            for r in range(4):
                for k in range(PLANES):
                    group = slice(k * PLANE_COLS, (k + 1) * PLANE_COLS)
                    nc.sync.dma_start(
                        out=planes[4 * k + r : P : 32, :, :].bitcast(I32),
                        in_=scales[group, r:16:4, :].rearrange("g q n -> q g n").bitcast(I32),
                    )

        h1_chunks = []
        w2_chunks = []
        w3_chunks = []

        def load_h1(c):
            h1_sb = acts.tile([P, CHUNK, HID], BF16)
            nc.sync.dma_start(out=h1_sb[:], in_=h1[:, c * CHUNK : (c + 1) * CHUNK, :])
            h1_chunks.append(h1_sb)

        def load_w2(c, pieces=1):
            w2_sb = weights.tile([P, CHUNK, PACK * HID], U8, align_bytes=64)
            size = CHUNK // pieces
            for first in range(0, CHUNK, size):
                nc.sync.dma_start(
                    out=w2_sb[:, first : first + size, :].bitcast(I32),
                    in_=W2_words[c * CHUNK + first : c * CHUNK + first + size]
                    .rearrange("g p n t -> p g (n t)")
                    .bitcast(I32),
                )
            w2_chunks.append(w2_sb)

        def load_w3(c):
            rows = slice(c * CHUNK, (c + 1) * CHUNK)
            w3_sb = weights.tile([P, CHUNK, PACK * FEAT], U8, align_bytes=64)
            nc.sync.dma_start(
                out=w3_sb[:].bitcast(I32),
                in_=W3_words[rows].rearrange("g p n t -> p g (n t)").bitcast(I32),
            )
            w3_chunks.append(w3_sb)

        def load_weights(c):
            load_w2(c)
            load_w3(c)

        b3_all = const.tile([P, NEURONS, FEAT], BF16)

        def load_b3(k):
            group = slice(k * PLANE_COLS, (k + 1) * PLANE_COLS)
            nc.sync.dma_start(
                out=b3_all[:, group, :].rearrange("p n d -> p (n d)"),
                in_=b3[group, :].rearrange("n d -> (n d)").partition_broadcast(P),
            )

        load_h1(0)
        load_scales(w2_planes, W2_scales)
        load_w2(0, pieces=2)
        load_scales(w3_planes, W3_scales)
        load_w3(0)
        load_b3(0)
        for c in range(1, N_CHUNKS):
            load_h1(c)
            load_weights(c)
            if c % 2 == 1 and c < N_CHUNKS - 1:
                load_b3((c + 1) // 2)

        affine_ps = psum.tile([P, HALVES, P], BF16, tag="xT", bufs=2)
        for half in range(HALVES):
            nc.tensor.transpose(
                out=affine_ps[:, half, :],
                in_=affine_rows[:, half * P : (half + 1) * P],
                identity=ident_bf16[:],
            )
        affine_cols = const.tile([P, HALVES, P], F32)
        nc.vector.tensor_copy(out=affine_cols[:], in_=affine_ps[:])

        bias_ps = psum.tile([P, PACK, P], F32, tag="xT", bufs=2)
        nc.tensor.transpose(out=bias_ps[:, 0, :], in_=bias_rows[:].bitcast(F32), identity=ident_f32[:])
        bias_cols = const.tile([P, P], F32)
        nc.vector.tensor_copy(out=bias_cols[:], in_=bias_ps[:, 0, :])
        b2_all = const.tile([P, NEURONS, HID], BF16)

        def spread(first_row, target, turn):
            spread_ps = psum.tile([P, PACK, P], F32, tag=("z", "ynT")[turn % 2])
            for q in range(PACK):
                nc.tensor.transpose(
                    out=spread_ps[:, q, :],
                    in_=bias_cols[:, first_row + q : first_row + q + 1].to_broadcast([P, P]),
                    identity=ident_f32[:],
                )
            words = target.bitcast(F32).rearrange("p n w -> p (n w)")
            if turn % 2 == 0:
                nc.scalar.copy(out=words, in_=spread_ps[:].rearrange("p q w -> p (q w)"))
            else:
                nc.vector.tensor_copy(out=words, in_=spread_ps[:].rearrange("p q w -> p (q w)"))

        spreads = []
        for c in range(N_CHUNKS):
            for i in (2 * c, 2 * c + 1):
                spreads.append((PACK * i, b2_all[:, PAIR * i : PAIR * (i + 1), :]))

        def spread_some(first, count):
            for turn in range(first, min(first + count, len(spreads))):
                spread(spreads[turn][0], spreads[turn][1], turn)

        spread_some(0, SPREAD_AHEAD)

        a_ops = {}
        x_biased = {}
        g_grouped = {}
        g_ops = {}
        y_biased = {}
        moments = {}
        y_norm = {}
        z_cols = {}
        out_tiles = {}

        def quantise_h1(i):
            h1_sb = h1_chunks[i // 2]
            a_ps = psum.tile([P, PAIR, 2, P], F32, tag="aT")
            for j in range(PAIR):
                words = h1_sb[:, (i % 2) * PAIR + j, :].bitcast(F32)
                for u in range(2):
                    nc.tensor.transpose(
                        out=a_ps[:, j, u, :], in_=words[:, u : HID // 2 : 2], identity=ident_f32[:]
                    )
            a_grouped = work.tile([P, PAIR * HID], BF16, align_bytes=64)
            nc.scalar.copy(
                out=a_grouped[:].bitcast(F32).rearrange("p (j b u) -> p j b u", j=PAIR, u=2),
                in_=a_ps[:].rearrange("p j u b -> p j b u"),
            )
            a_codes = work.tile([P, PAIR * P], U32, align_bytes=64, bufs=3)
            a_scales = work.tile([P, PAIR * P], U8, align_bytes=64, bufs=3)
            nc.vector.quantize_mx(out=a_codes[:].bitcast(FP8X4), scales=a_scales[:], in_=a_grouped[:])
            a_ops[i] = (a_codes, a_scales)

        def layer2(i):
            a_codes, a_scales = a_ops[i]
            xb = work.tile([P, PAIR, PACK, P], F32)
            for j in range(PAIR):
                n = i * PAIR + j
                rows = slice(j * P, (j + 1) * P)
                x2 = psum.tile([P, HID], F32, tag="x2", bufs=2)
                nc.tensor.matmul_mx(
                    out=x2[:],
                    lhsT=a_codes[:, rows].bitcast(FP8X4),
                    lhsT_scale=a_scales[:, rows],
                    rhs=w2_chunks[n // CHUNK][:, n % CHUNK, :].bitcast(FP8X4),
                    rhs_scale=w2_planes[4 * (n // PLANE_COLS) : P, n % PLANE_COLS, :],
                    start=True,
                    stop=True,
                )
                nc.vector.tensor_tensor(
                    out=xb[:, j, :, :],
                    in0=x2[:].rearrange("b (p t) -> b t p", t=PACK),
                    in1=b2_all[:, n, :].rearrange("b (p t) -> b t p", t=PACK),
                    op=ALU.add,
                )
            x_biased[i] = xb

        def gelu_transposed(i):
            xb = x_biased[i]
            gg = work.tile([P, PAIR, P, PACK], BF16, align_bytes=64)
            for j in range(PAIR):
                x_ps = psum.tile([P, PACK, P], F32, tag="xT", bufs=2)
                for t in range(PACK):
                    nc.tensor.transpose(out=x_ps[:, t, :], in_=xb[:, j, t, :], identity=ident_f32[:])
                nc.scalar.activation(
                    out=gg[:, j, :, :], in_=x_ps[:].rearrange("p t b -> p b t"), func=ACT.Gelu
                )
            g_grouped[i] = gg

        def quantise_g(i):
            g_codes = work.tile([P, PAIR * P], U32, align_bytes=64)
            g_scales = work.tile([P, PAIR * P], U8, align_bytes=64)
            nc.vector.quantize_mx(
                out=g_codes[:].bitcast(FP8X4),
                scales=g_scales[:],
                in_=g_grouped[i][:].rearrange("p j b t -> p (j b t)"),
            )
            g_ops[i] = (g_codes, g_scales)

        def layer3(i):
            g_codes, g_scales = g_ops[i]
            x3 = psum.tile([P, PAIR, FEAT], F32, tag="x3")
            for j in range(PAIR):
                n = i * PAIR + j
                rows = slice(j * P, (j + 1) * P)
                nc.tensor.matmul_mx(
                    out=x3[:, j, :],
                    lhsT=g_codes[:, rows].bitcast(FP8X4),
                    lhsT_scale=g_scales[:, rows],
                    rhs=w3_chunks[n // CHUNK][:, n % CHUNK, :].bitcast(FP8X4),
                    rhs_scale=w3_planes[4 * (n // PLANE_COLS) : P, n % PLANE_COLS, :],
                    start=True,
                    stop=True,
                )
            y = work.tile([P, PAIR, FEAT], F32, bufs=3)
            nc.vector.tensor_tensor(
                out=y[:], in0=x3[:], in1=b3_all[:, i * PAIR : (i + 1) * PAIR, :], op=ALU.add
            )
            y_biased[i] = y

        def statistics(i):
            stats = work.tile([P, PAIR, 3], F32, bufs=3)
            nc.vector.bn_stats(
                out=stats[:].rearrange("p j s -> p (j s)"), in_=y_biased[i][:].rearrange("p j d -> p d j")
            )
            var_eps = work.tile([P, PAIR], F32, bufs=3)
            nc.gpsimd.tensor_scalar(
                out=var_eps[:],
                in0=stats[:, :, 2],
                scalar1=1.0 / FEAT,
                scalar2=LN_EPS,
                op0=ALU.mult,
                op1=ALU.add,
            )
            rstd = work.tile([P, PAIR], F32, bufs=3)
            nc.gpsimd.tensor_tensor(out=rstd[:], in0=var_eps[:], in1=neg_half[:], op=ALU.pow)
            moments[i] = (y_biased[i], stats, rstd)

        def normalise(i):
            y, stats, rstd = moments[i]
            yn = work.tile([P, PAIR, FEAT], F32)
            for j in range(PAIR):
                nc.vector.tensor_scalar(
                    out=yn[:, j, :],
                    in0=y[:, j, :],
                    scalar1=stats[:, j, 1:2],
                    scalar2=rstd[:, j : j + 1],
                    op0=ALU.subtract,
                    op1=ALU.mult,
                )
            y_norm[i] = yn

        def scale_and_shift(i):
            yn = y_norm[i]
            yn_ps = psum.tile([P, PAIR, HALVES, P], F32, tag="ynT")
            zc = work.tile([P, PAIR, HALVES, P], F32)
            for j in range(PAIR):
                for half in range(HALVES):
                    nc.tensor.transpose(
                        out=yn_ps[:, j, half, :],
                        in_=yn[:, j, half * P : (half + 1) * P],
                        identity=ident_f32[:],
                    )
            for j in range(PAIR):
                n = i * PAIR + j
                for half in range(HALVES):
                    nc.scalar.activation(
                        out=zc[:, j, half, :],
                        in_=yn_ps[:, j, half, :],
                        func=ACT.Identity,
                        scale=affine_cols[:, half, n : n + 1],
                        bias=affine_cols[:, half, 32 + n : 32 + n + 1],
                    )
            z_cols[i] = zc

        def gain_and_store(i):
            zc = z_cols[i]
            c = i // 2
            if i % 2 == 0:
                out_sb = work.tile([P, CHUNK, FEAT], F32, bufs=3)
                out_tiles[c] = out_sb
            z_ps = psum.tile([P, PAIR, FEAT], F32, tag="z")
            for j in range(PAIR):
                for half in range(HALVES):
                    nc.tensor.transpose(
                        out=z_ps[:, j, half * P : (half + 1) * P],
                        in_=zc[:, j, half, :],
                        identity=ident_f32[:],
                    )
            for j in range(PAIR):
                n = i * PAIR + j
                nc.scalar.mul(
                    out=out_tiles[c][:, n % CHUNK, :], in_=z_ps[:, j, :], mul=oscillator_gain(n, tick)
                )
            if i % 2 == 1:
                nc.scalar.dma_start(out=out[:, c * CHUNK : (c + 1) * CHUNK, :], in_=out_tiles[c][:])

        def run(stage, i):
            if 0 <= i < N_PAIRS:
                stage(i)

        for step in range(N_PAIRS + 7):
            run(quantise_g, step - 3)
            run(statistics, step - 4)
            run(normalise, step - 5)
            run(quantise_h1, step)
            run(gain_and_store, step - 7)
            run(scale_and_shift, step - 6)
            run(gelu_transposed, step - 2)
            run(layer2, step - 1)
            run(layer3, step - 3)
            spread_some(SPREAD_AHEAD + SPREAD_A_STEP * step, SPREAD_A_STEP)
